import numpy as np
import ml_dtypes


def mxq(x, axis, fmt="e4m3"):
    dtype, down = {"e4m3": (ml_dtypes.float8_e4m3fn, 7), "e5m2": (ml_dtypes.float8_e5m2, 14)}[fmt]
    v = np.moveaxis(np.asarray(x, np.float32).astype(ml_dtypes.bfloat16).astype(np.float64), axis, -1)
    blocks = v.reshape(v.shape[:-1] + (-1, 32))
    amax = np.abs(blocks).max(-1, keepdims=True)
    byte = np.maximum(np.where(amax > 0, np.frexp(amax)[1] - 1 + 127, 0) - down, 1)
    scale = np.exp2(byte - 127.0)
    codes = (blocks / scale).astype(np.float32).astype(dtype).astype(np.float64)
    return np.moveaxis((codes * scale).reshape(v.shape), -1, axis)


WIDE = False


def mx_kscale(k):
    if not WIDE:
        return np.ones(k)
    levels = np.array([10, -10, 5, -5, 0])
    a = np.random.permutation(np.resize(levels, k // 512 * 4)).reshape(k // 512, 4)
    idx = np.arange(k)
    return np.exp2(a[idx // 512, idx % 128 // 32])


BF16 = ml_dtypes.bfloat16


def bf(x):
    return np.asarray(x, np.float32).astype(BF16)


def f64(x):
    return np.asarray(x).astype(np.float64)


B, H, E, V = 4096, 512, 512, 512


def sigmoid(v):
    return 1.0 / (1.0 + np.exp(-v))


def setup_inputs():
    s, t = mx_kscale(E), mx_kscale(H)
    return {
        "input_data": bf(np.random.standard_normal((B, E)) * s),
        "previous_hidden_state": bf(np.random.standard_normal((B, H)) * t),
        "c_t": bf(np.random.standard_normal((B, H)) * 0.7),
        "w_ip_o": bf(np.random.standard_normal((E, H)) / np.sqrt(E) / s[:, None]),
        "w_output": bf(np.random.standard_normal((H, H)) / np.sqrt(H) / t[:, None]),
        "w_output_c": bf(np.random.standard_normal((H, H)) / np.sqrt(H)),
        "w_op": bf(np.random.standard_normal((H, V)) * 3.0 / np.sqrt(H)),
    }


def reference(input_data, previous_hidden_state, c_t, w_ip_o, w_output, w_output_c, w_op):
    ct = f64(c_t)
    zo = (mxq(f64(input_data), 1, "e4m3") @ mxq(f64(w_ip_o), 0, "e4m3")) \
        + (mxq(f64(previous_hidden_state), 1, "e4m3") @ mxq(f64(w_output), 0, "e4m3"))
    ot = sigmoid(zo + (mxq(ct, 1, "e4m3") @ mxq(f64(w_output_c), 0, "e4m3")))
    ht = ot * np.tanh(ct)
    yt = sigmoid(mxq(ht, 1, "e4m3") @ mxq(f64(w_op), 0, "e4m3"))
    return yt, ht

@@ -1,0 +1,244 @@
+from contextlib import ExitStack
+
+import concourse.mybir as mybir
+from concourse.masks import make_identity
+
+F32 = mybir.dt.float32
+BF16 = mybir.dt.bfloat16
+U32 = mybir.dt.uint32
+U8 = mybir.dt.uint8
+FP8X4 = mybir.dt.float8_e4m3fn_x4
+ACT = mybir.ActivationFunctionType
+MULT = mybir.AluOpType.mult
+
+P = 128
+PACK = 4
+BATCH = 4096
+WIDTH = 512
+TILES = BATCH // P
+UNIT = 2
+UNITS = TILES // UNIT
+GATE_INPUTS = 3
+CELL = 2
+PAIR = 2
+HALVES = WIDTH // PAIR // P
+
+PREFETCH = 6
+HIDDEN_LAG = 3
+VECTOR_COLUMNS = 352
+
+FLOPS = 2 * BATCH * WIDTH * WIDTH * (GATE_INPUTS + 1)
+
+
+def tile_lstm_peephole_build_pb_t_kernel(
+    tc, input_data, previous_hidden_state, c_t, w_ip_o, w_output, w_output_c, w_op, out_0, out_1
+):
+    nc = tc.nc
+
+    def by_tile(dram):
+        return dram.rearrange("(p i) k -> p i k", i=TILES)
+
+    gate_inputs = [by_tile(input_data), by_tile(previous_hidden_state), by_tile(c_t)]
+    yt_dram = by_tile(out_0)
+    ht_dram = by_tile(out_1)
+
+    with ExitStack() as stack:
+        keep = stack.enter_context(tc.tile_pool(name="keep", bufs=1))
+        weight_stage = stack.enter_context(tc.tile_pool(name="weight_stage", bufs=2))
+        inputs = stack.enter_context(tc.tile_pool(name="inputs", bufs=PREFETCH + 2))
+        stage = stack.enter_context(tc.tile_pool(name="stage", bufs=2))
+        psum = stack.enter_context(tc.psum_pool(name="psum", bufs=8))
+        stack.enter_context(tc.manual_schedule())
+
+        loaded, input_banks, grouped_inputs, input_codes = {}, {}, {}, {}
+        tanh_cell, hidden, hidden_banks, grouped_hidden, hidden_codes, readout_banks = {}, {}, {}, {}, {}, {}
+
+        def in_range(u):
+            return 0 <= u < UNITS
+
+        def tiles_of(u):
+            return slice(u * UNIT, (u + 1) * UNIT)
+
+        def load_unit(u):
+            if not in_range(u):
+                return
+            x_sb = inputs.tile([P, UNIT, WIDTH], BF16)
+            h_sb = inputs.tile([P, UNIT, WIDTH], BF16)
+            c_sb = inputs.tile([P, UNIT, WIDTH], BF16)
+            loaded[u] = [x_sb, h_sb, c_sb]
+            for sbuf, dram in zip(loaded[u], gate_inputs):
+                nc.sync.dma_start(out=sbuf[:], in_=dram[:, tiles_of(u), :])
+
+        def load_weight(w, run):
+            raw = weight_stage.tile([P, PACK, WIDTH], BF16, bufs=GATE_INPUTS + 1)
+            nc.sync.dma_start(
+                out=raw[:].rearrange("p (u e) n -> p u e n", e=run),
+                in_=w.rearrange("(u p e) n -> p u e n", p=P, e=run),
+            )
+            return raw
+
+        def quantise_weight(raw, label):
+            grouped = weight_stage.tile([P, WIDTH, PACK], BF16, align_bytes=64)
+            turned = raw[:].rearrange("p t n -> p n t")
+            nc.vector.tensor_copy(out=grouped[:, :VECTOR_COLUMNS, :], in_=turned[:, :VECTOR_COLUMNS, :])
+            nc.scalar.copy(out=grouped[:, VECTOR_COLUMNS:, :], in_=turned[:, VECTOR_COLUMNS:, :])
+            codes = keep.tile([P, WIDTH], U32, name=label + "_codes", align_bytes=64)
+            scales = keep.tile([P, WIDTH], U8, name=label + "_scales", align_bytes=64)
+            nc.vector.quantize_mx(
+                out=codes[:].bitcast(FP8X4), scales=scales[:], in_=grouped[:].rearrange("p n t -> p (n t)")
+            )
+            return codes, scales
+
+        def transpose_inputs(u):
+            if not in_range(u):
+                return
+            input_banks[u] = []
+            for sbuf in loaded[u]:
+                words = sbuf[:].bitcast(F32)
+                bank = psum.tile([P, UNIT, HALVES, P], F32, tag="bank")
+                for a in range(UNIT):
+                    for half in range(HALVES):
+                        nc.tensor.transpose(
+                            out=bank[:, a, half, :], in_=words[:, a, half * P : (half + 1) * P], identity=identity[:]
+                        )
+                input_banks[u].append(bank)
+
+        def regroup_inputs(u):
+            if not in_range(u):
+                return
+            in_grouped = stage.tile([P, GATE_INPUTS, UNIT * P * PACK], BF16, align_bytes=64)
+            grouped_inputs[u] = in_grouped
+            tanh_c = stage.tile([P, UNIT, WIDTH], F32, bufs=3)
+            tanh_cell[u] = tanh_c
+            nc.scalar.activation(out=tanh_c[:], in_=loaded[u][CELL][:], func=ACT.Tanh)
+            for g in range(GATE_INPUTS):
+                copy = nc.scalar.copy if g == CELL else nc.vector.tensor_copy
+                copy(
+                    out=in_grouped[:, g, :].bitcast(F32).rearrange("p (a w half) -> p a w half", a=UNIT, half=HALVES),
+                    in_=input_banks[u][g][:].rearrange("p a half w -> p a w half"),
+                )
+
+        def quantise_inputs(u):
+            if not in_range(u):
+                return
+            in_codes = stage.tile([P, GATE_INPUTS, UNIT, P], U32, bufs=3, align_bytes=64)
+            in_scales = stage.tile([P, GATE_INPUTS, UNIT, P], U8, bufs=3, align_bytes=64)
+            input_codes[u] = (in_codes, in_scales)
+            for g in range(GATE_INPUTS):
+                nc.vector.quantize_mx(
+                    out=in_codes[:, g].rearrange("p a w -> p (a w)").bitcast(FP8X4),
+                    scales=in_scales[:, g].rearrange("p a w -> p (a w)"),
+                    in_=grouped_inputs[u][:, g, :],
+                )
+
+        def gate_and_hidden(u):
+            if not in_range(u):
+                return
+            codes, scales = input_codes[u]
+            gate = stage.tile([P, UNIT, WIDTH], F32)
+            ht = stage.tile([P, UNIT, WIDTH], F32, bufs=HIDDEN_LAG + 1)
+            hidden[u] = ht
+            for a in range(UNIT):
+                bank = psum.tile([P, WIDTH], F32, tag="bank")
+                for g in range(GATE_INPUTS):
+                    nc.tensor.matmul_mx(
+                        out=bank[:],
+                        lhsT=codes[:, g, a, :].bitcast(FP8X4),
+                        lhsT_scale=scales[:, g, a, :],
+                        rhs=gate_codes[g][0][:].bitcast(FP8X4),
+                        rhs_scale=gate_codes[g][1][:],
+                        start=(g == 0),
+                        stop=(g == GATE_INPUTS - 1),
+                    )
+                nc.scalar.activation(out=gate[:, a, :], in_=bank[:], func=ACT.Sigmoid)
+                nc.gpsimd.tensor_tensor(out=ht[:, a, :], in0=gate[:, a, :], in1=tanh_cell[u][:, a, :], op=MULT)
+            nc.sync.dma_start(out=ht_dram[:, tiles_of(u), :], in_=ht[:])
+
+        def transpose_hidden(u):
+            if not in_range(u):
+                return
+            hidden_banks[u] = []
+            for a in range(UNIT):
+                bank = psum.tile([P, PACK, P], F32, tag="bank")
+                for t in range(PACK):
+                    nc.tensor.transpose(
+                        out=bank[:, t, :], in_=hidden[u][:, a, t * P : (t + 1) * P], identity=identity[:]
+                    )
+                hidden_banks[u].append(bank)
+
+        def regroup_hidden(u):
+            if not in_range(u):
+                return
+            ht_grouped = stage.tile([P, UNIT, P, PACK], BF16, align_bytes=64)
+            grouped_hidden[u] = ht_grouped
+            for a in range(UNIT):
+                nc.vector.tensor_copy(out=ht_grouped[:, a], in_=hidden_banks[u][a][:].rearrange("p t w -> p w t"))
+
+        def quantise_hidden(u):
+            if not in_range(u):
+                return
+            ht_codes = stage.tile([P, UNIT, P], U32, align_bytes=64)
+            ht_scales = stage.tile([P, UNIT, P], U8, align_bytes=64)
+            hidden_codes[u] = (ht_codes, ht_scales)
+            nc.vector.quantize_mx(
+                out=ht_codes[:].rearrange("p a w -> p (a w)").bitcast(FP8X4),
+                scales=ht_scales[:].rearrange("p a w -> p (a w)"),
+                in_=grouped_hidden[u][:].rearrange("p a w t -> p (a w t)"),
+            )
+
+        def readout_matmuls(u):
+            if not in_range(u):
+                return
+            codes, scales = hidden_codes[u]
+            readout_banks[u] = []
+            for a in range(UNIT):
+                bank = psum.tile([P, WIDTH], F32, tag="bank")
+                nc.tensor.matmul_mx(
+                    out=bank[:],
+                    lhsT=codes[:, a, :].bitcast(FP8X4),
+                    lhsT_scale=scales[:, a, :],
+                    rhs=readout_codes[0][:].bitcast(FP8X4),
+                    rhs_scale=readout_codes[1][:],
+                    start=True,
+                    stop=True,
+                )
+                readout_banks[u].append(bank)
+
+        def readout(u):
+            if not in_range(u):
+                return
+            yt = stage.tile([P, UNIT, WIDTH], F32, bufs=3)
+            for a in range(UNIT):
+                nc.scalar.activation(out=yt[:, a, :], in_=readout_banks[u][a][:], func=ACT.Sigmoid)
+            nc.sync.dma_start(out=yt_dram[:, tiles_of(u), :], in_=yt[:])
+
+        def step(s):
+            load_unit(s + PREFETCH)
+            transpose_hidden(s - HIDDEN_LAG)
+            transpose_inputs(s)
+            readout(s - HIDDEN_LAG - 1)
+            regroup_hidden(s - HIDDEN_LAG)
+            regroup_inputs(s)
+            quantise_hidden(s - HIDDEN_LAG)
+            quantise_inputs(s)
+            gate_and_hidden(s - 1)
+            readout_matmuls(s - HIDDEN_LAG)
+
+        zero = keep.tile([P, 1], F32)
+        nc.vector.memset(zero[:], 0.0)
+        warm = keep.tile([P, 1], F32)
+        nc.scalar.activation(out=warm[:], in_=zero[:], func=ACT.Sigmoid)
+        identity = keep.tile([P, P], F32)
+        make_identity(nc, identity[:])
+
+        gate_raw = [load_weight(w, PAIR) for w in (w_ip_o, w_output, w_output_c)]
+        load_unit(0)
+        readout_raw = load_weight(w_op, 1)
+        for u in range(1, PREFETCH):
+            load_unit(u)
+
+        gate_codes = [quantise_weight(raw, "gate%d" % g) for g, raw in enumerate(gate_raw)]
+        step(0)
+        readout_codes = quantise_weight(readout_raw, "readout")
+        for s in range(1, UNITS + HIDDEN_LAG + 1):
+            step(s)

@@ -151,7 +151,8 @@ def tile_lstm_peephole_build_pb_t_kernel(
                         stop=(g == GATE_INPUTS - 1),
                     )
                 nc.scalar.activation(out=gate[:, a, :], in_=bank[:], func=ACT.Sigmoid)
-                nc.gpsimd.tensor_tensor(out=ht[:, a, :], in0=gate[:, a, :], in1=tanh_cell[u][:, a, :], op=MULT)
+                multiplier = nc.vector if a == 0 else nc.gpsimd
+                multiplier.tensor_tensor(out=ht[:, a, :], in0=gate[:, a, :], in1=tanh_cell[u][:, a, :], op=MULT)
             nc.sync.dma_start(out=ht_dram[:, tiles_of(u), :], in_=ht[:])
 
         def transpose_hidden(u):

@@ -51,7 +51,7 @@ def tile_lstm_peephole_build_pb_t_kernel(
         stack.enter_context(tc.manual_schedule())
 
         loaded, input_banks, grouped_inputs, input_codes = {}, {}, {}, {}
-        tanh_cell, hidden, hidden_banks, grouped_hidden, hidden_codes, readout_banks = {}, {}, {}, {}, {}, {}
+        tanh_cell, hidden, hidden_banks, grouped_hidden, hidden_codes = {}, {}, {}, {}, {}
 
         def in_range(u):
             return 0 <= u < UNITS
@@ -187,11 +187,11 @@ def tile_lstm_peephole_build_pb_t_kernel(
                 in_=grouped_hidden[u][:].rearrange("p a w t -> p (a w t)"),
             )
 
-        def readout_matmuls(u):
+        def readout(u):
             if not in_range(u):
                 return
             codes, scales = hidden_codes[u]
-            readout_banks[u] = []
+            yt = stage.tile([P, UNIT, WIDTH], F32, bufs=3)
             for a in range(UNIT):
                 bank = psum.tile([P, WIDTH], F32, tag="bank")
                 nc.tensor.matmul_mx(
@@ -203,27 +203,19 @@ def tile_lstm_peephole_build_pb_t_kernel(
                     start=True,
                     stop=True,
                 )
-                readout_banks[u].append(bank)
-
-        def readout(u):
-            if not in_range(u):
-                return
-            yt = stage.tile([P, UNIT, WIDTH], F32, bufs=3)
-            for a in range(UNIT):
-                nc.scalar.activation(out=yt[:, a, :], in_=readout_banks[u][a][:], func=ACT.Sigmoid)
+                nc.scalar.activation(out=yt[:, a, :], in_=bank[:], func=ACT.Sigmoid)
             nc.sync.dma_start(out=yt_dram[:, tiles_of(u), :], in_=yt[:])
 
         def step(s):
             load_unit(s + PREFETCH)
             transpose_hidden(s - HIDDEN_LAG)
             transpose_inputs(s)
-            readout(s - HIDDEN_LAG - 1)
             regroup_hidden(s - HIDDEN_LAG)
             regroup_inputs(s)
             quantise_hidden(s - HIDDEN_LAG)
             quantise_inputs(s)
+            readout(s - HIDDEN_LAG - 1)
             gate_and_hidden(s - 1)
-            readout_matmuls(s - HIDDEN_LAG)
 
         zero = keep.tile([P, 1], F32)
         nc.vector.memset(zero[:], 0.0)

@@ -18,16 +18,18 @@ WIDTH = 512
 TILES = BATCH // P
 UNIT = 2
 UNITS = TILES // UNIT
-GATE_INPUTS = 3
-CELL = 2
 PAIR = 2
 HALVES = WIDTH // PAIR // P
+GATE_INPUTS = 3
+CELL = 2
+HIDDEN = 3
+OPERANDS = 4
 
 PREFETCH = 6
 HIDDEN_LAG = 3
 VECTOR_COLUMNS = 352
 
-FLOPS = 2 * BATCH * WIDTH * WIDTH * (GATE_INPUTS + 1)
+FLOPS = 2 * BATCH * WIDTH * WIDTH * OPERANDS
 
 
 def tile_lstm_peephole_build_pb_t_kernel(
@@ -46,12 +48,12 @@ def tile_lstm_peephole_build_pb_t_kernel(
         keep = stack.enter_context(tc.tile_pool(name="keep", bufs=1))
         weight_stage = stack.enter_context(tc.tile_pool(name="weight_stage", bufs=2))
         inputs = stack.enter_context(tc.tile_pool(name="inputs", bufs=PREFETCH + 2))
-        stage = stack.enter_context(tc.tile_pool(name="stage", bufs=2))
+        stage = stack.enter_context(tc.tile_pool(name="stage", bufs=3))
         psum = stack.enter_context(tc.psum_pool(name="psum", bufs=8))
         stack.enter_context(tc.manual_schedule())
 
-        loaded, input_banks, grouped_inputs, input_codes = {}, {}, {}, {}
-        tanh_cell, hidden, hidden_banks, grouped_hidden, hidden_codes = {}, {}, {}, {}, {}
+        loaded, tanh_cell, gates, hidden, rounded_hidden = {}, {}, {}, {}, {}
+        banks, grouped, quantised = {}, {}, {}
 
         def in_range(u):
             return 0 <= u < UNITS
@@ -69,31 +71,38 @@ def tile_lstm_peephole_build_pb_t_kernel(
             for sbuf, dram in zip(loaded[u], gate_inputs):
                 nc.sync.dma_start(out=sbuf[:], in_=dram[:, tiles_of(u), :])
 
-        def load_weight(w, run):
-            raw = weight_stage.tile([P, PACK, WIDTH], BF16, bufs=GATE_INPUTS + 1)
+        def load_weight(w):
+            raw = weight_stage.tile([P, PACK, WIDTH], BF16, bufs=OPERANDS)
             nc.sync.dma_start(
-                out=raw[:].rearrange("p (u e) n -> p u e n", e=run),
-                in_=w.rearrange("(u p e) n -> p u e n", p=P, e=run),
+                out=raw[:].rearrange("p (u e) n -> p u e n", e=PAIR),
+                in_=w.rearrange("(u p e) n -> p u e n", p=P, e=PAIR),
             )
             return raw
 
         def quantise_weight(raw, label):
-            grouped = weight_stage.tile([P, WIDTH, PACK], BF16, align_bytes=64)
+            side_by_side = weight_stage.tile([P, WIDTH, PACK], BF16, align_bytes=64)
             turned = raw[:].rearrange("p t n -> p n t")
-            nc.vector.tensor_copy(out=grouped[:, :VECTOR_COLUMNS, :], in_=turned[:, :VECTOR_COLUMNS, :])
-            nc.scalar.copy(out=grouped[:, VECTOR_COLUMNS:, :], in_=turned[:, VECTOR_COLUMNS:, :])
+            nc.vector.tensor_copy(out=side_by_side[:, :VECTOR_COLUMNS, :], in_=turned[:, :VECTOR_COLUMNS, :])
+            nc.scalar.copy(out=side_by_side[:, VECTOR_COLUMNS:, :], in_=turned[:, VECTOR_COLUMNS:, :])
             codes = keep.tile([P, WIDTH], U32, name=label + "_codes", align_bytes=64)
             scales = keep.tile([P, WIDTH], U8, name=label + "_scales", align_bytes=64)
             nc.vector.quantize_mx(
-                out=codes[:].bitcast(FP8X4), scales=scales[:], in_=grouped[:].rearrange("p n t -> p (n t)")
+                out=codes[:].bitcast(FP8X4), scales=scales[:], in_=side_by_side[:].rearrange("p n t -> p (n t)")
             )
             return codes, scales
 
-        def transpose_inputs(u):
-            if not in_range(u):
-                return
-            input_banks[u] = []
-            for sbuf in loaded[u]:
+        def operands_of(s):
+            found = {}
+            if in_range(s):
+                for g in range(GATE_INPUTS):
+                    found[g] = loaded[s][g]
+            if in_range(s - HIDDEN_LAG):
+                found[HIDDEN] = rounded_hidden[s - HIDDEN_LAG]
+            return found
+
+        def transpose_operands(s):
+            banks[s] = {}
+            for g, sbuf in operands_of(s).items():
                 words = sbuf[:].bitcast(F32)
                 bank = psum.tile([P, UNIT, HALVES, P], F32, tag="bank")
                 for a in range(UNIT):
@@ -101,121 +110,95 @@ def tile_lstm_peephole_build_pb_t_kernel(
                         nc.tensor.transpose(
                             out=bank[:, a, half, :], in_=words[:, a, half * P : (half + 1) * P], identity=identity[:]
                         )
-                input_banks[u].append(bank)
+                banks[s][g] = bank
 
-        def regroup_inputs(u):
-            if not in_range(u):
+        def regroup_operands(s):
+            if not banks[s]:
                 return
-            in_grouped = stage.tile([P, GATE_INPUTS, UNIT * P * PACK], BF16, align_bytes=64)
-            grouped_inputs[u] = in_grouped
-            tanh_c = stage.tile([P, UNIT, WIDTH], F32, bufs=3)
-            tanh_cell[u] = tanh_c
-            nc.scalar.activation(out=tanh_c[:], in_=loaded[u][CELL][:], func=ACT.Tanh)
-            for g in range(GATE_INPUTS):
+            side_by_side = stage.tile([P, OPERANDS, UNIT * P * PACK], BF16, bufs=2, align_bytes=64)
+            grouped[s] = side_by_side
+            if in_range(s):
+                tanh_c = stage.tile([P, UNIT, WIDTH], F32, bufs=4)
+                tanh_cell[s] = tanh_c
+                nc.scalar.activation(out=tanh_c[:], in_=loaded[s][CELL][:], func=ACT.Tanh)
+            for g, bank in banks[s].items():
                 copy = nc.scalar.copy if g == CELL else nc.vector.tensor_copy
                 copy(
-                    out=in_grouped[:, g, :].bitcast(F32).rearrange("p (a w half) -> p a w half", a=UNIT, half=HALVES),
-                    in_=input_banks[u][g][:].rearrange("p a half w -> p a w half"),
+                    out=side_by_side[:, g, :].bitcast(F32).rearrange("p (a w half) -> p a w half", a=UNIT, half=HALVES),
+                    in_=bank[:].rearrange("p a half w -> p a w half"),
                 )
 
-        def quantise_inputs(u):
-            if not in_range(u):
+        def quantise_operands(s):
+            if not banks[s]:
                 return
-            in_codes = stage.tile([P, GATE_INPUTS, UNIT, P], U32, bufs=3, align_bytes=64)
-            in_scales = stage.tile([P, GATE_INPUTS, UNIT, P], U8, bufs=3, align_bytes=64)
-            input_codes[u] = (in_codes, in_scales)
-            for g in range(GATE_INPUTS):
+            codes = stage.tile([P, OPERANDS, UNIT, P], U32, align_bytes=64)
+            scales = stage.tile([P, OPERANDS, UNIT, P], U8, align_bytes=64)
+            quantised[s] = (codes, scales)
+            for g in banks[s]:
                 nc.vector.quantize_mx(
-                    out=in_codes[:, g].rearrange("p a w -> p (a w)").bitcast(FP8X4),
-                    scales=in_scales[:, g].rearrange("p a w -> p (a w)"),
-                    in_=grouped_inputs[u][:, g, :],
+                    out=codes[:, g].rearrange("p a w -> p (a w)").bitcast(FP8X4),
+                    scales=scales[:, g].rearrange("p a w -> p (a w)"),
+                    in_=grouped[s][:, g, :],
                 )
 
-        def gate_and_hidden(u):
+        def multiply(bank, s, g, a, start, stop):
+            codes, scales = quantised[s]
+            nc.tensor.matmul_mx(
+                out=bank[:],
+                lhsT=codes[:, g, a, :].bitcast(FP8X4),
+                lhsT_scale=scales[:, g, a, :],
+                rhs=weights[g][0][:].bitcast(FP8X4),
+                rhs_scale=weights[g][1][:],
+                start=start,
+                stop=stop,
+            )
+
+        def gate(u):
             if not in_range(u):
                 return
-            codes, scales = input_codes[u]
-            gate = stage.tile([P, UNIT, WIDTH], F32)
-            ht = stage.tile([P, UNIT, WIDTH], F32, bufs=HIDDEN_LAG + 1)
+            gate_sb = stage.tile([P, UNIT, WIDTH], F32)
+            ht = stage.tile([P, UNIT, WIDTH], F32)
+            gates[u] = gate_sb
             hidden[u] = ht
             for a in range(UNIT):
                 bank = psum.tile([P, WIDTH], F32, tag="bank")
                 for g in range(GATE_INPUTS):
-                    nc.tensor.matmul_mx(
-                        out=bank[:],
-                        lhsT=codes[:, g, a, :].bitcast(FP8X4),
-                        lhsT_scale=scales[:, g, a, :],
-                        rhs=gate_codes[g][0][:].bitcast(FP8X4),
-                        rhs_scale=gate_codes[g][1][:],
-                        start=(g == 0),
-                        stop=(g == GATE_INPUTS - 1),
-                    )
-                nc.scalar.activation(out=gate[:, a, :], in_=bank[:], func=ACT.Sigmoid)
-                multiplier = nc.vector if a == 0 else nc.gpsimd
-                multiplier.tensor_tensor(out=ht[:, a, :], in0=gate[:, a, :], in1=tanh_cell[u][:, a, :], op=MULT)
-            nc.sync.dma_start(out=ht_dram[:, tiles_of(u), :], in_=ht[:])
+                    multiply(bank, u, g, a, start=(g == 0), stop=(g == GATE_INPUTS - 1))
+                nc.scalar.activation(out=gate_sb[:, a, :], in_=bank[:], func=ACT.Sigmoid)
+            nc.gpsimd.tensor_tensor(out=ht[:, 1, :], in0=gate_sb[:, 1, :], in1=tanh_cell[u][:, 1, :], op=MULT)
 
-        def transpose_hidden(u):
+        def first_product(u):
             if not in_range(u):
                 return
-            hidden_banks[u] = []
-            for a in range(UNIT):
-                bank = psum.tile([P, PACK, P], F32, tag="bank")
-                for t in range(PACK):
-                    nc.tensor.transpose(
-                        out=bank[:, t, :], in_=hidden[u][:, a, t * P : (t + 1) * P], identity=identity[:]
-                    )
-                hidden_banks[u].append(bank)
+            nc.vector.tensor_tensor(out=hidden[u][:, 0, :], in0=gates[u][:, 0, :], in1=tanh_cell[u][:, 0, :], op=MULT)
 
-        def regroup_hidden(u):
+        def round_hidden(u):
             if not in_range(u):
                 return
-            ht_grouped = stage.tile([P, UNIT, P, PACK], BF16, align_bytes=64)
-            grouped_hidden[u] = ht_grouped
-            for a in range(UNIT):
-                nc.vector.tensor_copy(out=ht_grouped[:, a], in_=hidden_banks[u][a][:].rearrange("p t w -> p w t"))
-
-        def quantise_hidden(u):
-            if not in_range(u):
-                return
-            ht_codes = stage.tile([P, UNIT, P], U32, align_bytes=64)
-            ht_scales = stage.tile([P, UNIT, P], U8, align_bytes=64)
-            hidden_codes[u] = (ht_codes, ht_scales)
-            nc.vector.quantize_mx(
-                out=ht_codes[:].rearrange("p a w -> p (a w)").bitcast(FP8X4),
-                scales=ht_scales[:].rearrange("p a w -> p (a w)"),
-                in_=grouped_hidden[u][:].rearrange("p a w t -> p (a w t)"),
-            )
+            ht16 = stage.tile([P, UNIT, WIDTH], BF16)
+            rounded_hidden[u] = ht16
+            nc.vector.tensor_copy(out=ht16[:], in_=hidden[u][:])
+            nc.sync.dma_start(out=ht_dram[:, tiles_of(u), :], in_=hidden[u][:])
 
         def readout(u):
             if not in_range(u):
                 return
-            codes, scales = hidden_codes[u]
-            yt = stage.tile([P, UNIT, WIDTH], F32, bufs=3)
+            yt = stage.tile([P, UNIT, WIDTH], F32)
             for a in range(UNIT):
                 bank = psum.tile([P, WIDTH], F32, tag="bank")
-                nc.tensor.matmul_mx(
-                    out=bank[:],
-                    lhsT=codes[:, a, :].bitcast(FP8X4),
-                    lhsT_scale=scales[:, a, :],
-                    rhs=readout_codes[0][:].bitcast(FP8X4),
-                    rhs_scale=readout_codes[1][:],
-                    start=True,
-                    stop=True,
-                )
+                multiply(bank, u + HIDDEN_LAG, HIDDEN, a, start=True, stop=True)
                 nc.scalar.activation(out=yt[:, a, :], in_=bank[:], func=ACT.Sigmoid)
             nc.sync.dma_start(out=yt_dram[:, tiles_of(u), :], in_=yt[:])
 
         def step(s):
             load_unit(s + PREFETCH)
-            transpose_hidden(s - HIDDEN_LAG)
-            transpose_inputs(s)
-            regroup_hidden(s - HIDDEN_LAG)
-            regroup_inputs(s)
-            quantise_hidden(s - HIDDEN_LAG)
-            quantise_inputs(s)
-            readout(s - HIDDEN_LAG - 1)
-            gate_and_hidden(s - 1)
+            transpose_operands(s)
+            first_product(s - 2)
+            regroup_operands(s)
+            round_hidden(s - 2)
+            quantise_operands(s)
+            readout(s - 1 - HIDDEN_LAG)
+            gate(s - 1)
 
         zero = keep.tile([P, 1], F32)
         nc.vector.memset(zero[:], 0.0)
@@ -224,14 +207,14 @@ def tile_lstm_peephole_build_pb_t_kernel(
         identity = keep.tile([P, P], F32)
         make_identity(nc, identity[:])
 
-        gate_raw = [load_weight(w, PAIR) for w in (w_ip_o, w_output, w_output_c)]
+        raw_weights = [load_weight(w) for w in (w_ip_o, w_output, w_output_c)]
         load_unit(0)
-        readout_raw = load_weight(w_op, 1)
+        raw_weights.append(load_weight(w_op))
         for u in range(1, PREFETCH):
             load_unit(u)
 
-        gate_codes = [quantise_weight(raw, "gate%d" % g) for g, raw in enumerate(gate_raw)]
+        weights = [quantise_weight(raw_weights[g], "weight%d" % g) for g in range(GATE_INPUTS)]
         step(0)
-        readout_codes = quantise_weight(readout_raw, "readout")
+        weights.append(quantise_weight(raw_weights[HIDDEN], "weight%d" % HIDDEN))
         for s in range(1, UNITS + HIDDEN_LAG + 1):
             step(s)

@@ -25,7 +25,10 @@ CELL = 2
 HIDDEN = 3
 OPERANDS = 4
 
-PREFETCH = 6
+LOAD_UNITS = 2
+LOADS = UNITS // LOAD_UNITS
+PREFETCH = 4
+STORE_BUFS = 5
 HIDDEN_LAG = 3
 VECTOR_COLUMNS = 352
 
@@ -47,7 +50,7 @@ def tile_lstm_peephole_build_pb_t_kernel(
     with ExitStack() as stack:
         keep = stack.enter_context(tc.tile_pool(name="keep", bufs=1))
         weight_stage = stack.enter_context(tc.tile_pool(name="weight_stage", bufs=2))
-        inputs = stack.enter_context(tc.tile_pool(name="inputs", bufs=PREFETCH + 2))
+        inputs = stack.enter_context(tc.tile_pool(name="inputs", bufs=PREFETCH + 1))
         stage = stack.enter_context(tc.tile_pool(name="stage", bufs=3))
         psum = stack.enter_context(tc.psum_pool(name="psum", bufs=8))
         stack.enter_context(tc.manual_schedule())
@@ -61,15 +64,22 @@ def tile_lstm_peephole_build_pb_t_kernel(
         def tiles_of(u):
             return slice(u * UNIT, (u + 1) * UNIT)
 
-        def load_unit(u):
-            if not in_range(u):
+        def load(j, parts=1):
+            if j >= LOADS:
                 return
-            x_sb = inputs.tile([P, UNIT, WIDTH], BF16)
-            h_sb = inputs.tile([P, UNIT, WIDTH], BF16)
-            c_sb = inputs.tile([P, UNIT, WIDTH], BF16)
-            loaded[u] = [x_sb, h_sb, c_sb]
-            for sbuf, dram in zip(loaded[u], gate_inputs):
-                nc.sync.dma_start(out=sbuf[:], in_=dram[:, tiles_of(u), :])
+            x_sb = inputs.tile([P, LOAD_UNITS, UNIT, WIDTH], BF16)
+            h_sb = inputs.tile([P, LOAD_UNITS, UNIT, WIDTH], BF16)
+            c_sb = inputs.tile([P, LOAD_UNITS, UNIT, WIDTH], BF16)
+            for v in range(LOAD_UNITS):
+                loaded[j * LOAD_UNITS + v] = [sbuf[:, v, :, :] for sbuf in (x_sb, h_sb, c_sb)]
+            piece = LOAD_UNITS // parts
+            for i in range(parts):
+                u = j * LOAD_UNITS + i * piece
+                for sbuf, dram in zip((x_sb, h_sb, c_sb), gate_inputs):
+                    nc.sync.dma_start(
+                        out=sbuf[:, i * piece : (i + 1) * piece, :, :].rearrange("p v a k -> p (v a) k"),
+                        in_=dram[:, u * UNIT : (u + piece) * UNIT, :],
+                    )
 
         def load_weight(w):
             raw = weight_stage.tile([P, PACK, WIDTH], BF16, bufs=OPERANDS)
@@ -103,7 +113,7 @@ def tile_lstm_peephole_build_pb_t_kernel(
         def transpose_operands(s):
             banks[s] = {}
             for g, sbuf in operands_of(s).items():
-                words = sbuf[:].bitcast(F32)
+                words = sbuf.bitcast(F32)
                 bank = psum.tile([P, UNIT, HALVES, P], F32, tag="bank")
                 for a in range(UNIT):
                     for half in range(HALVES):
@@ -120,7 +130,7 @@ def tile_lstm_peephole_build_pb_t_kernel(
             if in_range(s):
                 tanh_c = stage.tile([P, UNIT, WIDTH], F32, bufs=4)
                 tanh_cell[s] = tanh_c
-                nc.scalar.activation(out=tanh_c[:], in_=loaded[s][CELL][:], func=ACT.Tanh)
+                nc.scalar.activation(out=tanh_c[:], in_=loaded[s][CELL], func=ACT.Tanh)
             for g, bank in banks[s].items():
                 copy = nc.scalar.copy if g == CELL else nc.vector.tensor_copy
                 copy(
@@ -157,7 +167,7 @@ def tile_lstm_peephole_build_pb_t_kernel(
             if not in_range(u):
                 return
             gate_sb = stage.tile([P, UNIT, WIDTH], F32)
-            ht = stage.tile([P, UNIT, WIDTH], F32)
+            ht = stage.tile([P, UNIT, WIDTH], F32, bufs=STORE_BUFS)
             gates[u] = gate_sb
             hidden[u] = ht
             for a in range(UNIT):
@@ -176,14 +186,14 @@ def tile_lstm_peephole_build_pb_t_kernel(
             if not in_range(u):
                 return
             ht16 = stage.tile([P, UNIT, WIDTH], BF16)
-            rounded_hidden[u] = ht16
+            rounded_hidden[u] = ht16[:]
             nc.vector.tensor_copy(out=ht16[:], in_=hidden[u][:])
             nc.sync.dma_start(out=ht_dram[:, tiles_of(u), :], in_=hidden[u][:])
 
         def readout(u):
             if not in_range(u):
                 return
-            yt = stage.tile([P, UNIT, WIDTH], F32)
+            yt = stage.tile([P, UNIT, WIDTH], F32, bufs=STORE_BUFS)
             for a in range(UNIT):
                 bank = psum.tile([P, WIDTH], F32, tag="bank")
                 multiply(bank, u + HIDDEN_LAG, HIDDEN, a, start=True, stop=True)
@@ -191,7 +201,8 @@ def tile_lstm_peephole_build_pb_t_kernel(
             nc.sync.dma_start(out=yt_dram[:, tiles_of(u), :], in_=yt[:])
 
         def step(s):
-            load_unit(s + PREFETCH)
+            if s % LOAD_UNITS == 0:
+                load(s // LOAD_UNITS + PREFETCH)
             transpose_operands(s)
             first_product(s - 2)
             regroup_operands(s)
@@ -208,10 +219,10 @@ def tile_lstm_peephole_build_pb_t_kernel(
         make_identity(nc, identity[:])
 
         raw_weights = [load_weight(w) for w in (w_ip_o, w_output, w_output_c)]
-        load_unit(0)
+        load(0, parts=LOAD_UNITS)
         raw_weights.append(load_weight(w_op))
-        for u in range(1, PREFETCH):
-            load_unit(u)
+        for j in range(1, PREFETCH):
+            load(j)
 
         weights = [quantise_weight(raw_weights[g], "weight%d" % g) for g in range(GATE_INPUTS)]
         step(0)

@@ -30,6 +30,7 @@ LOADS = UNITS // LOAD_UNITS
 PREFETCH = 4
 STORE_BUFS = 5
 HIDDEN_LAG = 3
+VECTOR_PRODUCT = 384
 VECTOR_COLUMNS = 352
 
 FLOPS = 2 * BATCH * WIDTH * WIDTH * OPERANDS
@@ -57,6 +58,9 @@ def tile_lstm_peephole_build_pb_t_kernel(
 
         loaded, tanh_cell, gates, hidden, rounded_hidden = {}, {}, {}, {}, {}
         banks, grouped, quantised = {}, {}, {}
+
+        def flat(tile):
+            return tile[:].rearrange("p a n -> p (a n)")
 
         def in_range(u):
             return 0 <= u < UNITS
@@ -175,12 +179,22 @@ def tile_lstm_peephole_build_pb_t_kernel(
                 for g in range(GATE_INPUTS):
                     multiply(bank, u, g, a, start=(g == 0), stop=(g == GATE_INPUTS - 1))
                 nc.scalar.activation(out=gate_sb[:, a, :], in_=bank[:], func=ACT.Sigmoid)
-            nc.gpsimd.tensor_tensor(out=ht[:, 1, :], in0=gate_sb[:, 1, :], in1=tanh_cell[u][:, 1, :], op=MULT)
+            nc.gpsimd.tensor_tensor(
+                out=flat(ht)[:, VECTOR_PRODUCT:],
+                in0=flat(gate_sb)[:, VECTOR_PRODUCT:],
+                in1=flat(tanh_cell[u])[:, VECTOR_PRODUCT:],
+                op=MULT,
+            )
 
         def first_product(u):
             if not in_range(u):
                 return
-            nc.vector.tensor_tensor(out=hidden[u][:, 0, :], in0=gates[u][:, 0, :], in1=tanh_cell[u][:, 0, :], op=MULT)
+            nc.vector.tensor_tensor(
+                out=flat(hidden[u])[:, :VECTOR_PRODUCT],
+                in0=flat(gates[u])[:, :VECTOR_PRODUCT],
+                in1=flat(tanh_cell[u])[:, :VECTOR_PRODUCT],
+                op=MULT,
+            )
 
         def round_hidden(u):
             if not in_range(u):

@@ -222,8 +222,8 @@ def tile_lstm_peephole_build_pb_t_kernel(
             regroup_operands(s)
             round_hidden(s - 2)
             quantise_operands(s)
-            readout(s - 1 - HIDDEN_LAG)
             gate(s - 1)
+            readout(s - 1 - HIDDEN_LAG)
 
         zero = keep.tile([P, 1], F32)
         nc.vector.memset(zero[:], 0.0)

@@ -10,14 +10,17 @@ U8 = mybir.dt.uint8
 FP8X4 = mybir.dt.float8_e4m3fn_x4
 ACT = mybir.ActivationFunctionType
 MULT = mybir.AluOpType.mult
+VECTOR_PRODUCT = 192
 
 P = 128
 PACK = 4
 BATCH = 4096
 WIDTH = 512
 TILES = BATCH // P
-UNIT = 2
-UNITS = TILES // UNIT
+END_V = 0
+UNIT_TILES = [2] * 15 + [1] * 2
+UNITS = len(UNIT_TILES)
+UNIT_START = [sum(UNIT_TILES[:u]) for u in range(UNITS)]
 PAIR = 2
 HALVES = WIDTH // PAIR // P
 GATE_INPUTS = 3
@@ -25,12 +28,18 @@ CELL = 2
 HIDDEN = 3
 OPERANDS = 4
 
-LOAD_UNITS = 2
-LOADS = UNITS // LOAD_UNITS
-PREFETCH = 4
+LOAD_TILES = [2, 2] + [4] * 7
+LOADS = len(LOAD_TILES)
+LOAD_START = [sum(LOAD_TILES[:j]) for j in range(LOADS)]
+MAX_TILES = max(UNIT_TILES)
+STORE_UNITS = [1] * UNITS
+STORE_FIRST = [sum(STORE_UNITS[:i]) for i in range(len(STORE_UNITS))]
+STORE_OF = [first for first, count in zip(STORE_FIRST, STORE_UNITS) for unit in range(count)]
+STORE_LAST = [first + count - 1 for first, count in zip(STORE_FIRST, STORE_UNITS)]
+STORE_TILES = [sum(UNIT_TILES[v] for v in range(UNITS) if STORE_OF[v] == STORE_OF[u]) for u in range(UNITS)]
+PREFETCH = 16
 STORE_BUFS = 5
 HIDDEN_LAG = 3
-VECTOR_PRODUCT = 384
 VECTOR_COLUMNS = 352
 
 FLOPS = 2 * BATCH * WIDTH * WIDTH * OPERANDS
@@ -51,39 +60,49 @@ def tile_lstm_peephole_build_pb_t_kernel(
     with ExitStack() as stack:
         keep = stack.enter_context(tc.tile_pool(name="keep", bufs=1))
         weight_stage = stack.enter_context(tc.tile_pool(name="weight_stage", bufs=2))
-        inputs = stack.enter_context(tc.tile_pool(name="inputs", bufs=PREFETCH + 1))
+        inputs = stack.enter_context(tc.tile_pool(name="inputs", bufs=6))
         stage = stack.enter_context(tc.tile_pool(name="stage", bufs=3))
         psum = stack.enter_context(tc.psum_pool(name="psum", bufs=8))
         stack.enter_context(tc.manual_schedule())
 
         loaded, tanh_cell, gates, hidden, rounded_hidden = {}, {}, {}, {}, {}
         banks, grouped, quantised = {}, {}, {}
+        gate_banks, readout_banks = {}, {}
+        issued = set()
 
         def flat(tile):
-            return tile[:].rearrange("p a n -> p (a n)")
+            return tile.rearrange("p a n -> p (a n)")
+
+        open_store = {}
+
+        def hidden_rows(u):
+            tile, first = hidden[u]
+            return tile[:, first : first + UNIT_TILES[u], :]
+
+        def store_tiles(u):
+            first = UNIT_START[STORE_OF[u]]
+            return slice(first, UNIT_START[u] + UNIT_TILES[u])
+
+        def vector_columns(u):
+            return UNIT_TILES[u] * WIDTH if u >= UNITS - END_V else UNIT_TILES[u] * VECTOR_PRODUCT
 
         def in_range(u):
             return 0 <= u < UNITS
 
         def tiles_of(u):
-            return slice(u * UNIT, (u + 1) * UNIT)
+            return slice(UNIT_START[u], UNIT_START[u] + UNIT_TILES[u])
 
-        def load(j, parts=1):
-            if j >= LOADS:
-                return
-            x_sb = inputs.tile([P, LOAD_UNITS, UNIT, WIDTH], BF16)
-            h_sb = inputs.tile([P, LOAD_UNITS, UNIT, WIDTH], BF16)
-            c_sb = inputs.tile([P, LOAD_UNITS, UNIT, WIDTH], BF16)
-            for v in range(LOAD_UNITS):
-                loaded[j * LOAD_UNITS + v] = [sbuf[:, v, :, :] for sbuf in (x_sb, h_sb, c_sb)]
-            piece = LOAD_UNITS // parts
-            for i in range(parts):
-                u = j * LOAD_UNITS + i * piece
-                for sbuf, dram in zip((x_sb, h_sb, c_sb), gate_inputs):
-                    nc.sync.dma_start(
-                        out=sbuf[:, i * piece : (i + 1) * piece, :, :].rearrange("p v a k -> p (v a) k"),
-                        in_=dram[:, u * UNIT : (u + piece) * UNIT, :],
-                    )
+        def load(j):
+            first, count = LOAD_START[j], LOAD_TILES[j]
+            x_sb = inputs.tile([P, count, WIDTH], BF16)
+            h_sb = inputs.tile([P, count, WIDTH], BF16)
+            c_sb = inputs.tile([P, count, WIDTH], BF16)
+            for sbuf, dram in zip((x_sb, h_sb, c_sb), gate_inputs):
+                nc.sync.dma_start(out=sbuf[:], in_=dram[:, first : first + count, :])
+            for u in range(UNITS):
+                a = UNIT_START[u] - first
+                if 0 <= a < count:
+                    loaded[u] = [sbuf[:, a : a + UNIT_TILES[u], :] for sbuf in (x_sb, h_sb, c_sb)]
 
         def load_weight(w):
             raw = weight_stage.tile([P, PACK, WIDTH], BF16, bufs=OPERANDS)
@@ -111,49 +130,87 @@ def tile_lstm_peephole_build_pb_t_kernel(
                 for g in range(GATE_INPUTS):
                     found[g] = loaded[s][g]
             if in_range(s - HIDDEN_LAG):
-                found[HIDDEN] = rounded_hidden[s - HIDDEN_LAG]
+                found[HIDDEN] = rounded_hidden[s - HIDDEN_LAG][:] if s - HIDDEN_LAG in rounded_hidden else None
             return found
 
-        def transpose_operands(s):
-            banks[s] = {}
+        def transpose_operands(s, which):
+            banks.setdefault(s, {})
             for g, sbuf in operands_of(s).items():
+                if g not in which:
+                    continue
                 words = sbuf.bitcast(F32)
-                bank = psum.tile([P, UNIT, HALVES, P], F32, tag="bank")
-                for a in range(UNIT):
+                tiles = words.shape[1]
+                bank = psum.tile([P, tiles, HALVES, P], F32, tag="bank")
+                for a in range(tiles):
                     for half in range(HALVES):
                         nc.tensor.transpose(
                             out=bank[:, a, half, :], in_=words[:, a, half * P : (half + 1) * P], identity=identity[:]
                         )
                 banks[s][g] = bank
 
-        def regroup_operands(s):
-            if not banks[s]:
+        def open_step(s):
+            if not operands_of(s):
                 return
-            side_by_side = stage.tile([P, OPERANDS, UNIT * P * PACK], BF16, bufs=2, align_bytes=64)
-            grouped[s] = side_by_side
-            if in_range(s):
-                tanh_c = stage.tile([P, UNIT, WIDTH], F32, bufs=4)
-                tanh_cell[s] = tanh_c
-                nc.scalar.activation(out=tanh_c[:], in_=loaded[s][CELL], func=ACT.Tanh)
-            for g, bank in banks[s].items():
-                copy = nc.scalar.copy if g == CELL else nc.vector.tensor_copy
-                copy(
-                    out=side_by_side[:, g, :].bitcast(F32).rearrange("p (a w half) -> p a w half", a=UNIT, half=HALVES),
-                    in_=bank[:].rearrange("p a half w -> p a w half"),
-                )
-
-        def quantise_operands(s):
-            if not banks[s]:
-                return
-            codes = stage.tile([P, OPERANDS, UNIT, P], U32, align_bytes=64)
-            scales = stage.tile([P, OPERANDS, UNIT, P], U8, align_bytes=64)
+            grouped[s] = stage.tile([P, OPERANDS, MAX_TILES * P * PACK], BF16, name="side_by_side", bufs=2, align_bytes=64)
+            codes = stage.tile([P, OPERANDS, MAX_TILES, P], U32, align_bytes=64)
+            scales = stage.tile([P, OPERANDS, MAX_TILES, P], U8, align_bytes=64)
             quantised[s] = (codes, scales)
-            for g in banks[s]:
-                nc.vector.quantize_mx(
-                    out=codes[:, g].rearrange("p a w -> p (a w)").bitcast(FP8X4),
-                    scales=scales[:, g].rearrange("p a w -> p (a w)"),
-                    in_=grouped[s][:, g, :],
-                )
+
+        def tanh(u):
+            if not in_range(u):
+                return
+            tanh_c = stage.tile([P, UNIT_TILES[u], WIDTH], F32, bufs=4)
+            tanh_cell[u] = tanh_c
+            nc.scalar.activation(out=tanh_c[:], in_=loaded[u][CELL], func=ACT.Tanh)
+
+        def regroup(s, g, copy, rows=slice(0, P)):
+            bank = banks[s].get(g)
+            if bank is None:
+                return
+            tiles = bank.shape[1]
+            copy(
+                out=grouped[s][:, g, : tiles * P * PACK].bitcast(F32).rearrange(
+                    "p (a w half) -> p a w half", a=tiles, half=HALVES
+                )[:, :, rows, :],
+                in_=bank[:].rearrange("p a half w -> p a w half")[:, :, rows, :],
+            )
+
+        def quantise(s, g):
+            bank = banks[s].get(g)
+            if bank is None:
+                return
+            codes, scales = quantised[s]
+            tiles = bank.shape[1]
+            nc.vector.quantize_mx(
+                out=codes[:, g, :tiles].rearrange("p a w -> p (a w)").bitcast(FP8X4),
+                scales=scales[:, g, :tiles].rearrange("p a w -> p (a w)"),
+                in_=grouped[s][:, g, : tiles * P * PACK],
+            )
+
+        def quantise_all(s):
+            if any(banks[s].get(g) is None or banks[s][g].shape[1] < MAX_TILES for g in range(OPERANDS)):
+                for g in range(OPERANDS):
+                    quantise(s, g)
+                return
+            codes, scales = quantised[s]
+            nc.vector.quantize_mx(
+                out=codes[:].rearrange("p g a w -> p (g a w)").bitcast(FP8X4),
+                scales=scales[:].rearrange("p g a w -> p (g a w)"),
+                in_=grouped[s][:].rearrange("p g n -> p (g n)"),
+            )
+
+        def quantise_pair(s, g):
+            pair = [banks[s].get(g), banks[s].get(g + 1)]
+            if None in pair or pair[0].shape[1] < MAX_TILES or pair[1].shape[1] < MAX_TILES:
+                quantise(s, g)
+                quantise(s, g + 1)
+                return
+            codes, scales = quantised[s]
+            nc.vector.quantize_mx(
+                out=codes[:, g : g + 2].rearrange("p g a w -> p (g a w)").bitcast(FP8X4),
+                scales=scales[:, g : g + 2].rearrange("p g a w -> p (g a w)"),
+                in_=grouped[s][:, g : g + 2, :].rearrange("p g n -> p (g n)"),
+            )
 
         def multiply(bank, s, g, a, start, stop):
             codes, scales = quantised[s]
@@ -167,63 +224,93 @@ def tile_lstm_peephole_build_pb_t_kernel(
                 stop=stop,
             )
 
-        def gate(u):
+        def gate_passes(u, tiles=slice(0, MAX_TILES)):
             if not in_range(u):
                 return
-            gate_sb = stage.tile([P, UNIT, WIDTH], F32)
-            ht = stage.tile([P, UNIT, WIDTH], F32, bufs=STORE_BUFS)
-            gates[u] = gate_sb
-            hidden[u] = ht
-            for a in range(UNIT):
+            gate_banks.setdefault(u, [])
+            for a in range(UNIT_TILES[u])[tiles]:
                 bank = psum.tile([P, WIDTH], F32, tag="bank")
+                gate_banks[u].append(bank)
                 for g in range(GATE_INPUTS):
                     multiply(bank, u, g, a, start=(g == 0), stop=(g == GATE_INPUTS - 1))
+
+        def gate_sigmoid(u):
+            if not in_range(u):
+                return
+            gate_sb = stage.tile([P, UNIT_TILES[u], WIDTH], F32)
+            gates[u] = gate_sb
+            if u in STORE_FIRST:
+                open_store["ht"] = stage.tile([P, STORE_TILES[u], WIDTH], F32, name="ht", bufs=STORE_BUFS)
+            hidden[u] = (open_store["ht"], UNIT_START[u] - UNIT_START[STORE_OF[u]])
+            for a, bank in enumerate(gate_banks[u]):
                 nc.scalar.activation(out=gate_sb[:, a, :], in_=bank[:], func=ACT.Sigmoid)
-            nc.gpsimd.tensor_tensor(
-                out=flat(ht)[:, VECTOR_PRODUCT:],
-                in0=flat(gate_sb)[:, VECTOR_PRODUCT:],
-                in1=flat(tanh_cell[u])[:, VECTOR_PRODUCT:],
-                op=MULT,
-            )
+            if vector_columns(u) < UNIT_TILES[u] * WIDTH:
+                nc.gpsimd.tensor_tensor(
+                    out=flat(hidden_rows(u))[:, vector_columns(u) :],
+                    in0=flat(gate_sb[:])[:, vector_columns(u) :],
+                    in1=flat(tanh_cell[u][:])[:, vector_columns(u) :],
+                    op=MULT,
+                )
 
         def first_product(u):
             if not in_range(u):
                 return
             nc.vector.tensor_tensor(
-                out=flat(hidden[u])[:, :VECTOR_PRODUCT],
-                in0=flat(gates[u])[:, :VECTOR_PRODUCT],
-                in1=flat(tanh_cell[u])[:, :VECTOR_PRODUCT],
+                out=flat(hidden_rows(u))[:, : vector_columns(u)],
+                in0=flat(gates[u][:])[:, : vector_columns(u)],
+                in1=flat(tanh_cell[u][:])[:, : vector_columns(u)],
                 op=MULT,
             )
 
         def round_hidden(u):
             if not in_range(u):
                 return
-            ht16 = stage.tile([P, UNIT, WIDTH], BF16)
-            rounded_hidden[u] = ht16[:]
-            nc.vector.tensor_copy(out=ht16[:], in_=hidden[u][:])
-            nc.sync.dma_start(out=ht_dram[:, tiles_of(u), :], in_=hidden[u][:])
+            ht16 = stage.tile([P, UNIT_TILES[u], WIDTH], BF16)
+            rounded_hidden[u] = ht16
+            nc.vector.tensor_copy(out=ht16[:], in_=hidden_rows(u))
+            if u in STORE_LAST:
+                nc.sync.dma_start(out=ht_dram[:, store_tiles(u), :], in_=hidden[u][0][:])
 
-        def readout(u):
+        def readout_passes(u):
             if not in_range(u):
                 return
-            yt = stage.tile([P, UNIT, WIDTH], F32, bufs=STORE_BUFS)
-            for a in range(UNIT):
+            readout_banks[u] = []
+            for a in range(UNIT_TILES[u]):
                 bank = psum.tile([P, WIDTH], F32, tag="bank")
+                readout_banks[u].append(bank)
                 multiply(bank, u + HIDDEN_LAG, HIDDEN, a, start=True, stop=True)
-                nc.scalar.activation(out=yt[:, a, :], in_=bank[:], func=ACT.Sigmoid)
-            nc.sync.dma_start(out=yt_dram[:, tiles_of(u), :], in_=yt[:])
+
+        def readout_sigmoid(u):
+            if not in_range(u):
+                return
+            if u in STORE_FIRST:
+                open_store["yt"] = stage.tile([P, STORE_TILES[u], WIDTH], F32, name="yt", bufs=STORE_BUFS)
+            first = UNIT_START[u] - UNIT_START[STORE_OF[u]]
+            for a, bank in enumerate(readout_banks[u]):
+                nc.scalar.activation(out=open_store["yt"][:, first + a, :], in_=bank[:], func=ACT.Sigmoid)
+            if u in STORE_LAST:
+                nc.sync.dma_start(out=yt_dram[:, store_tiles(u), :], in_=open_store["yt"][:])
 
         def step(s):
-            if s % LOAD_UNITS == 0:
-                load(s // LOAD_UNITS + PREFETCH)
-            transpose_operands(s)
+            for j in range(LOADS):
+                if in_range(s) and j not in issued and LOAD_START[j] < UNIT_START[s] + PREFETCH:
+                    issued.add(j)
+                    load(j)
+            transpose_operands(s, range(OPERANDS))
+            open_step(s)
+            tanh(s)
             first_product(s - 2)
-            regroup_operands(s)
+            regroup(s, CELL, nc.scalar.copy)
+            regroup(s, 0, nc.vector.tensor_copy)
+            regroup(s, 1, nc.vector.tensor_copy)
+            regroup(s, HIDDEN, nc.vector.tensor_copy)
+            quantise_pair(s, 0)
             round_hidden(s - 2)
-            quantise_operands(s)
-            gate(s - 1)
-            readout(s - 1 - HIDDEN_LAG)
+            quantise_pair(s, CELL)
+            gate_passes(s - 1)
+            readout_passes(s - 1 - HIDDEN_LAG)
+            gate_sigmoid(s - 1)
+            readout_sigmoid(s - 1 - HIDDEN_LAG)
 
         zero = keep.tile([P, 1], F32)
         nc.vector.memset(zero[:], 0.0)
@@ -232,14 +319,20 @@ def tile_lstm_peephole_build_pb_t_kernel(
         identity = keep.tile([P, P], F32)
         make_identity(nc, identity[:])
 
-        raw_weights = [load_weight(w) for w in (w_ip_o, w_output, w_output_c)]
-        load(0, parts=LOAD_UNITS)
-        raw_weights.append(load_weight(w_op))
-        for j in range(1, PREFETCH):
-            load(j)
-
-        weights = [quantise_weight(raw_weights[g], "weight%d" % g) for g in range(GATE_INPUTS)]
+        raw = {}
+        raw[0] = load_weight((w_ip_o, w_output, w_output_c, w_op)[0])
+        raw[1] = load_weight((w_ip_o, w_output, w_output_c, w_op)[1])
+        raw[2] = load_weight((w_ip_o, w_output, w_output_c, w_op)[2])
+        load(0)
+        raw[3] = load_weight((w_ip_o, w_output, w_output_c, w_op)[3])
+        load(1)
+        issued.update((0, 1,))
+        weights = []
+        weights.append(quantise_weight(raw[0], "weight0"))
+        weights.append(quantise_weight(raw[1], "weight1"))
+        weights.append(quantise_weight(raw[2], "weight2"))
         step(0)
-        weights.append(quantise_weight(raw_weights[HIDDEN], "weight%d" % HIDDEN))
-        for s in range(1, UNITS + HIDDEN_LAG + 1):
+        weights.append(quantise_weight(raw[3], "weight3"))
+        step(1)
+        for s in range(2, UNITS + HIDDEN_LAG + 1):
             step(s)

@@ -28,7 +28,7 @@ CELL = 2
 HIDDEN = 3
 OPERANDS = 4
 
-LOAD_TILES = [2, 2] + [4] * 7
+LOAD_TILES = [2] * 4 + [4] * 6
 LOADS = len(LOAD_TILES)
 LOAD_START = [sum(LOAD_TILES[:j]) for j in range(LOADS)]
 MAX_TILES = max(UNIT_TILES)
@@ -40,7 +40,7 @@ STORE_TILES = [sum(UNIT_TILES[v] for v in range(UNITS) if STORE_OF[v] == STORE_O
 PREFETCH = 16
 STORE_BUFS = 5
 HIDDEN_LAG = 3
-VECTOR_COLUMNS = 352
+VECTOR_COLUMNS = 256
 
 FLOPS = 2 * BATCH * WIDTH * WIDTH * OPERANDS
 
@@ -60,7 +60,7 @@ def tile_lstm_peephole_build_pb_t_kernel(
     with ExitStack() as stack:
         keep = stack.enter_context(tc.tile_pool(name="keep", bufs=1))
         weight_stage = stack.enter_context(tc.tile_pool(name="weight_stage", bufs=2))
-        inputs = stack.enter_context(tc.tile_pool(name="inputs", bufs=6))
+        inputs = stack.enter_context(tc.tile_pool(name="inputs", bufs=7))
         stage = stack.enter_context(tc.tile_pool(name="stage", bufs=3))
         psum = stack.enter_context(tc.psum_pool(name="psum", bufs=8))
         stack.enter_context(tc.manual_schedule())
@@ -69,6 +69,7 @@ def tile_lstm_peephole_build_pb_t_kernel(
         banks, grouped, quantised = {}, {}, {}
         gate_banks, readout_banks = {}, {}
         issued = set()
+        raw, grouped_weights, weights = {}, {}, {}
 
         def flat(tile):
             return tile.rearrange("p a n -> p (a n)")
@@ -112,17 +113,22 @@ def tile_lstm_peephole_build_pb_t_kernel(
             )
             return raw
 
-        def quantise_weight(raw, label):
-            side_by_side = weight_stage.tile([P, WIDTH, PACK], BF16, align_bytes=64)
-            turned = raw[:].rearrange("p t n -> p n t")
+        def regroup_weight(w):
+            side_by_side = weight_stage.tile([P, WIDTH, PACK], BF16, bufs=3, align_bytes=64)
+            turned = raw[w][:].rearrange("p t n -> p n t")
             nc.vector.tensor_copy(out=side_by_side[:, :VECTOR_COLUMNS, :], in_=turned[:, :VECTOR_COLUMNS, :])
             nc.scalar.copy(out=side_by_side[:, VECTOR_COLUMNS:, :], in_=turned[:, VECTOR_COLUMNS:, :])
-            codes = keep.tile([P, WIDTH], U32, name=label + "_codes", align_bytes=64)
-            scales = keep.tile([P, WIDTH], U8, name=label + "_scales", align_bytes=64)
+            grouped_weights[w] = side_by_side
+
+        def quantise_weight(w):
+            codes = keep.tile([P, WIDTH], U32, name="codes%d" % w, align_bytes=64)
+            scales = keep.tile([P, WIDTH], U8, name="scales%d" % w, align_bytes=64)
             nc.vector.quantize_mx(
-                out=codes[:].bitcast(FP8X4), scales=scales[:], in_=side_by_side[:].rearrange("p n t -> p (n t)")
+                out=codes[:].bitcast(FP8X4),
+                scales=scales[:],
+                in_=grouped_weights[w][:].rearrange("p n t -> p (n t)"),
             )
-            return codes, scales
+            weights[w] = (codes, scales)
 
         def operands_of(s):
             found = {}
@@ -253,7 +259,7 @@ def tile_lstm_peephole_build_pb_t_kernel(
                 )
 
         def first_product(u):
-            if not in_range(u):
+            if not in_range(u) or vector_columns(u) == 0:
                 return
             nc.vector.tensor_tensor(
                 out=flat(hidden_rows(u))[:, : vector_columns(u)],
@@ -279,6 +285,11 @@ def tile_lstm_peephole_build_pb_t_kernel(
                 bank = psum.tile([P, WIDTH], F32, tag="bank")
                 readout_banks[u].append(bank)
                 multiply(bank, u + HIDDEN_LAG, HIDDEN, a, start=True, stop=True)
+
+        def keep_warm(count):
+            bank = psum.tile([P, WIDTH], F32, tag="bank")
+            for i in range(count):
+                nc.tensor.matmul(out=bank[:], lhsT=zeros[:, :P], rhs=zeros[:], start=True, stop=True)
 
         def readout_sigmoid(u):
             if not in_range(u):
@@ -312,6 +323,8 @@ def tile_lstm_peephole_build_pb_t_kernel(
             gate_sigmoid(s - 1)
             readout_sigmoid(s - 1 - HIDDEN_LAG)
 
+        zeros = keep.tile([P, WIDTH], BF16)
+        nc.gpsimd.memset(zeros[:], 0.0)
         zero = keep.tile([P, 1], F32)
         nc.vector.memset(zero[:], 0.0)
         warm = keep.tile([P, 1], F32)
@@ -319,20 +332,23 @@ def tile_lstm_peephole_build_pb_t_kernel(
         identity = keep.tile([P, P], F32)
         make_identity(nc, identity[:])
 
-        raw = {}
         raw[0] = load_weight((w_ip_o, w_output, w_output_c, w_op)[0])
         raw[1] = load_weight((w_ip_o, w_output, w_output_c, w_op)[1])
         raw[2] = load_weight((w_ip_o, w_output, w_output_c, w_op)[2])
         load(0)
-        raw[3] = load_weight((w_ip_o, w_output, w_output_c, w_op)[3])
         load(1)
+        raw[3] = load_weight((w_ip_o, w_output, w_output_c, w_op)[3])
         issued.update((0, 1,))
-        weights = []
-        weights.append(quantise_weight(raw[0], "weight0"))
-        weights.append(quantise_weight(raw[1], "weight1"))
-        weights.append(quantise_weight(raw[2], "weight2"))
+        regroup_weight(0)
+        regroup_weight(1)
+        quantise_weight(0)
+        regroup_weight(2)
+        quantise_weight(1)
+        quantise_weight(2)
         step(0)
-        weights.append(quantise_weight(raw[3], "weight3"))
         step(1)
-        for s in range(2, UNITS + HIDDEN_LAG + 1):
+        regroup_weight(3)
+        step(2)
+        quantise_weight(3)
+        for s in range(3, UNITS + HIDDEN_LAG + 1):
             step(s)

@@ -17,7 +17,7 @@ PACK = 4
 BATCH = 4096
 WIDTH = 512
 TILES = BATCH // P
-END_V = 0
+END_V = 1
 UNIT_TILES = [2] * 15 + [1] * 2
 UNITS = len(UNIT_TILES)
 UNIT_START = [sum(UNIT_TILES[:u]) for u in range(UNITS)]
@@ -37,8 +37,9 @@ STORE_FIRST = [sum(STORE_UNITS[:i]) for i in range(len(STORE_UNITS))]
 STORE_OF = [first for first, count in zip(STORE_FIRST, STORE_UNITS) for unit in range(count)]
 STORE_LAST = [first + count - 1 for first, count in zip(STORE_FIRST, STORE_UNITS)]
 STORE_TILES = [sum(UNIT_TILES[v] for v in range(UNITS) if STORE_OF[v] == STORE_OF[u]) for u in range(UNITS)]
-PREFETCH = 16
+PREFETCH = 12
 STORE_BUFS = 5
+HIDDEN_BUFS = 13
 HIDDEN_LAG = 3
 VECTOR_COLUMNS = 256
 
@@ -60,7 +61,7 @@ def tile_lstm_peephole_build_pb_t_kernel(
     with ExitStack() as stack:
         keep = stack.enter_context(tc.tile_pool(name="keep", bufs=1))
         weight_stage = stack.enter_context(tc.tile_pool(name="weight_stage", bufs=2))
-        inputs = stack.enter_context(tc.tile_pool(name="inputs", bufs=7))
+        inputs = stack.enter_context(tc.tile_pool(name="inputs", bufs=5))
         stage = stack.enter_context(tc.tile_pool(name="stage", bufs=3))
         psum = stack.enter_context(tc.psum_pool(name="psum", bufs=8))
         stack.enter_context(tc.manual_schedule())
@@ -246,7 +247,7 @@ def tile_lstm_peephole_build_pb_t_kernel(
             gate_sb = stage.tile([P, UNIT_TILES[u], WIDTH], F32)
             gates[u] = gate_sb
             if u in STORE_FIRST:
-                open_store["ht"] = stage.tile([P, STORE_TILES[u], WIDTH], F32, name="ht", bufs=STORE_BUFS)
+                open_store["ht"] = stage.tile([P, STORE_TILES[u], WIDTH], F32, name="ht", bufs=HIDDEN_BUFS)
             hidden[u] = (open_store["ht"], UNIT_START[u] - UNIT_START[STORE_OF[u]])
             for a, bank in enumerate(gate_banks[u]):
                 nc.scalar.activation(out=gate_sb[:, a, :], in_=bank[:], func=ACT.Sigmoid)
@@ -299,7 +300,9 @@ def tile_lstm_peephole_build_pb_t_kernel(
             first = UNIT_START[u] - UNIT_START[STORE_OF[u]]
             for a, bank in enumerate(readout_banks[u]):
                 nc.scalar.activation(out=open_store["yt"][:, first + a, :], in_=bank[:], func=ACT.Sigmoid)
-            if u in STORE_LAST:
+                if u >= UNITS - 4:
+                    nc.sync.dma_start(out=yt_dram[:, UNIT_START[u] + a : UNIT_START[u] + a + 1, :], in_=open_store["yt"][:, a : a + 1, :])
+            if u in STORE_LAST and u < UNITS - 4:
                 nc.sync.dma_start(out=yt_dram[:, store_tiles(u), :], in_=open_store["yt"][:])
 
         def step(s):

@@ -37,9 +37,8 @@ STORE_FIRST = [sum(STORE_UNITS[:i]) for i in range(len(STORE_UNITS))]
 STORE_OF = [first for first, count in zip(STORE_FIRST, STORE_UNITS) for unit in range(count)]
 STORE_LAST = [first + count - 1 for first, count in zip(STORE_FIRST, STORE_UNITS)]
 STORE_TILES = [sum(UNIT_TILES[v] for v in range(UNITS) if STORE_OF[v] == STORE_OF[u]) for u in range(UNITS)]
-PREFETCH = 12
+PREFETCH = 8
 STORE_BUFS = 5
-HIDDEN_BUFS = 13
 HIDDEN_LAG = 3
 VECTOR_COLUMNS = 256
 
@@ -61,7 +60,7 @@ def tile_lstm_peephole_build_pb_t_kernel(
     with ExitStack() as stack:
         keep = stack.enter_context(tc.tile_pool(name="keep", bufs=1))
         weight_stage = stack.enter_context(tc.tile_pool(name="weight_stage", bufs=2))
-        inputs = stack.enter_context(tc.tile_pool(name="inputs", bufs=5))
+        inputs = stack.enter_context(tc.tile_pool(name="inputs", bufs=4))
         stage = stack.enter_context(tc.tile_pool(name="stage", bufs=3))
         psum = stack.enter_context(tc.psum_pool(name="psum", bufs=8))
         stack.enter_context(tc.manual_schedule())
@@ -159,8 +158,8 @@ def tile_lstm_peephole_build_pb_t_kernel(
             if not operands_of(s):
                 return
             grouped[s] = stage.tile([P, OPERANDS, MAX_TILES * P * PACK], BF16, name="side_by_side", bufs=2, align_bytes=64)
-            codes = stage.tile([P, OPERANDS, MAX_TILES, P], U32, align_bytes=64)
-            scales = stage.tile([P, OPERANDS, MAX_TILES, P], U8, align_bytes=64)
+            codes = stage.tile([P, OPERANDS, MAX_TILES, P], U32, bufs=2, align_bytes=64)
+            scales = stage.tile([P, OPERANDS, MAX_TILES, P], U8, bufs=2, align_bytes=64)
             quantised[s] = (codes, scales)
 
         def tanh(u):
@@ -247,7 +246,7 @@ def tile_lstm_peephole_build_pb_t_kernel(
             gate_sb = stage.tile([P, UNIT_TILES[u], WIDTH], F32)
             gates[u] = gate_sb
             if u in STORE_FIRST:
-                open_store["ht"] = stage.tile([P, STORE_TILES[u], WIDTH], F32, name="ht", bufs=HIDDEN_BUFS)
+                open_store["ht"] = stage.tile([P, STORE_TILES[u], WIDTH], F32, name="ht", bufs=17)
             hidden[u] = (open_store["ht"], UNIT_START[u] - UNIT_START[STORE_OF[u]])
             for a, bank in enumerate(gate_banks[u]):
                 nc.scalar.activation(out=gate_sb[:, a, :], in_=bank[:], func=ACT.Sigmoid)
@@ -272,7 +271,7 @@ def tile_lstm_peephole_build_pb_t_kernel(
         def round_hidden(u):
             if not in_range(u):
                 return
-            ht16 = stage.tile([P, UNIT_TILES[u], WIDTH], BF16)
+            ht16 = stage.tile([P, UNIT_TILES[u], WIDTH], BF16, bufs=2)
             rounded_hidden[u] = ht16
             nc.vector.tensor_copy(out=ht16[:], in_=hidden_rows(u))
             if u in STORE_LAST:
@@ -296,7 +295,7 @@ def tile_lstm_peephole_build_pb_t_kernel(
             if not in_range(u):
                 return
             if u in STORE_FIRST:
-                open_store["yt"] = stage.tile([P, STORE_TILES[u], WIDTH], F32, name="yt", bufs=STORE_BUFS)
+                open_store["yt"] = stage.tile([P, STORE_TILES[u], WIDTH], F32, name="yt", bufs=6)
             first = UNIT_START[u] - UNIT_START[STORE_OF[u]]
             for a, bank in enumerate(readout_banks[u]):
                 nc.scalar.activation(out=open_store["yt"][:, first + a, :], in_=bank[:], func=ACT.Sigmoid)

from contextlib import ExitStack

import concourse.mybir as mybir
from concourse.masks import make_identity

F32 = mybir.dt.float32
BF16 = mybir.dt.bfloat16
U32 = mybir.dt.uint32
U8 = mybir.dt.uint8
FP8X4 = mybir.dt.float8_e4m3fn_x4
ACT = mybir.ActivationFunctionType
MULT = mybir.AluOpType.mult
VECTOR_PRODUCT = 192

P = 128
PACK = 4
BATCH = 4096
WIDTH = 512
TILES = BATCH // P
END_V = 1
UNIT_TILES = [2] * 15 + [1] * 2
UNITS = len(UNIT_TILES)
UNIT_START = [sum(UNIT_TILES[:u]) for u in range(UNITS)]
PAIR = 2
HALVES = WIDTH // PAIR // P
GATE_INPUTS = 3
CELL = 2
HIDDEN = 3
OPERANDS = 4

LOAD_TILES = [2] * 4 + [4] * 6
LOADS = len(LOAD_TILES)
LOAD_START = [sum(LOAD_TILES[:j]) for j in range(LOADS)]
MAX_TILES = max(UNIT_TILES)
STORE_UNITS = [1] * UNITS
STORE_FIRST = [sum(STORE_UNITS[:i]) for i in range(len(STORE_UNITS))]
STORE_OF = [first for first, count in zip(STORE_FIRST, STORE_UNITS) for unit in range(count)]
STORE_LAST = [first + count - 1 for first, count in zip(STORE_FIRST, STORE_UNITS)]
STORE_TILES = [sum(UNIT_TILES[v] for v in range(UNITS) if STORE_OF[v] == STORE_OF[u]) for u in range(UNITS)]
PREFETCH = 8
STORE_BUFS = 5
HIDDEN_LAG = 3
VECTOR_COLUMNS = 256

FLOPS = 2 * BATCH * WIDTH * WIDTH * OPERANDS


def tile_lstm_peephole_build_pb_t_kernel(
    tc, input_data, previous_hidden_state, c_t, w_ip_o, w_output, w_output_c, w_op, out_0, out_1
):
    nc = tc.nc

    def by_tile(dram):
        return dram.rearrange("(p i) k -> p i k", i=TILES)

    gate_inputs = [by_tile(input_data), by_tile(previous_hidden_state), by_tile(c_t)]
    yt_dram = by_tile(out_0)
    ht_dram = by_tile(out_1)

    with ExitStack() as stack:
        keep = stack.enter_context(tc.tile_pool(name="keep", bufs=1))
        weight_stage = stack.enter_context(tc.tile_pool(name="weight_stage", bufs=2))
        inputs = stack.enter_context(tc.tile_pool(name="inputs", bufs=4))
        stage = stack.enter_context(tc.tile_pool(name="stage", bufs=3))
        psum = stack.enter_context(tc.psum_pool(name="psum", bufs=8))
        stack.enter_context(tc.manual_schedule())

        loaded, tanh_cell, gates, hidden, rounded_hidden = {}, {}, {}, {}, {}
        banks, grouped, quantised = {}, {}, {}
        gate_banks, readout_banks = {}, {}
        issued = set()
        raw, grouped_weights, weights = {}, {}, {}

        def flat(tile):
            return tile.rearrange("p a n -> p (a n)")

        open_store = {}

        def hidden_rows(u):
            tile, first = hidden[u]
            return tile[:, first : first + UNIT_TILES[u], :]

        def store_tiles(u):
            first = UNIT_START[STORE_OF[u]]
            return slice(first, UNIT_START[u] + UNIT_TILES[u])

        def vector_columns(u):
            return UNIT_TILES[u] * WIDTH if u >= UNITS - END_V else UNIT_TILES[u] * VECTOR_PRODUCT

        def in_range(u):
            return 0 <= u < UNITS

        def tiles_of(u):
            return slice(UNIT_START[u], UNIT_START[u] + UNIT_TILES[u])

        def load(j):
            first, count = LOAD_START[j], LOAD_TILES[j]
            x_sb = inputs.tile([P, count, WIDTH], BF16)
            h_sb = inputs.tile([P, count, WIDTH], BF16)
            c_sb = inputs.tile([P, count, WIDTH], BF16)
            for sbuf, dram in zip((x_sb, h_sb, c_sb), gate_inputs):
                nc.sync.dma_start(out=sbuf[:], in_=dram[:, first : first + count, :])
            for u in range(UNITS):
                a = UNIT_START[u] - first
                if 0 <= a < count:
                    loaded[u] = [sbuf[:, a : a + UNIT_TILES[u], :] for sbuf in (x_sb, h_sb, c_sb)]

        def load_weight(w):
            raw = weight_stage.tile([P, PACK, WIDTH], BF16, bufs=OPERANDS)
            nc.sync.dma_start(
                out=raw[:].rearrange("p (u e) n -> p u e n", e=PAIR),
                in_=w.rearrange("(u p e) n -> p u e n", p=P, e=PAIR),
            )
            return raw

        def regroup_weight(w):
            side_by_side = weight_stage.tile([P, WIDTH, PACK], BF16, bufs=3, align_bytes=64)
            turned = raw[w][:].rearrange("p t n -> p n t")
            nc.vector.tensor_copy(out=side_by_side[:, :VECTOR_COLUMNS, :], in_=turned[:, :VECTOR_COLUMNS, :])
            nc.scalar.copy(out=side_by_side[:, VECTOR_COLUMNS:, :], in_=turned[:, VECTOR_COLUMNS:, :])
            grouped_weights[w] = side_by_side

        def quantise_weight(w):
            codes = keep.tile([P, WIDTH], U32, name="codes%d" % w, align_bytes=64)
            scales = keep.tile([P, WIDTH], U8, name="scales%d" % w, align_bytes=64)
            nc.vector.quantize_mx(
                out=codes[:].bitcast(FP8X4),
                scales=scales[:],
                in_=grouped_weights[w][:].rearrange("p n t -> p (n t)"),
            )
            weights[w] = (codes, scales)

        def operands_of(s):
            found = {}
            if in_range(s):
                for g in range(GATE_INPUTS):
                    found[g] = loaded[s][g]
            if in_range(s - HIDDEN_LAG):
                found[HIDDEN] = rounded_hidden[s - HIDDEN_LAG][:] if s - HIDDEN_LAG in rounded_hidden else None
            return found

        def transpose_operands(s, which):
            banks.setdefault(s, {})
            for g, sbuf in operands_of(s).items():
                if g not in which:
                    continue
                words = sbuf.bitcast(F32)
                tiles = words.shape[1]
                bank = psum.tile([P, tiles, HALVES, P], F32, tag="bank")
                for a in range(tiles):
                    for half in range(HALVES):
                        nc.tensor.transpose(
                            out=bank[:, a, half, :], in_=words[:, a, half * P : (half + 1) * P], identity=identity[:]
                        )
                banks[s][g] = bank

        def open_step(s):
            if not operands_of(s):
                return
            grouped[s] = stage.tile([P, OPERANDS, MAX_TILES * P * PACK], BF16, name="side_by_side", bufs=2, align_bytes=64)
            codes = stage.tile([P, OPERANDS, MAX_TILES, P], U32, bufs=2, align_bytes=64)
            scales = stage.tile([P, OPERANDS, MAX_TILES, P], U8, bufs=2, align_bytes=64)
            quantised[s] = (codes, scales)

        def tanh(u):
            if not in_range(u):
                return
            tanh_c = stage.tile([P, UNIT_TILES[u], WIDTH], F32, bufs=4)
            tanh_cell[u] = tanh_c
            nc.scalar.activation(out=tanh_c[:], in_=loaded[u][CELL], func=ACT.Tanh)

        def regroup(s, g, copy, rows=slice(0, P)):
            bank = banks[s].get(g)
            if bank is None:
                return
            tiles = bank.shape[1]
            copy(
                out=grouped[s][:, g, : tiles * P * PACK].bitcast(F32).rearrange(
                    "p (a w half) -> p a w half", a=tiles, half=HALVES
                )[:, :, rows, :],
                in_=bank[:].rearrange("p a half w -> p a w half")[:, :, rows, :],
            )

        def quantise(s, g):
            bank = banks[s].get(g)
            if bank is None:
                return
            codes, scales = quantised[s]
            tiles = bank.shape[1]
            nc.vector.quantize_mx(
                out=codes[:, g, :tiles].rearrange("p a w -> p (a w)").bitcast(FP8X4),
                scales=scales[:, g, :tiles].rearrange("p a w -> p (a w)"),
                in_=grouped[s][:, g, : tiles * P * PACK],
            )

        def quantise_all(s):
            if any(banks[s].get(g) is None or banks[s][g].shape[1] < MAX_TILES for g in range(OPERANDS)):
                for g in range(OPERANDS):
                    quantise(s, g)
                return
            codes, scales = quantised[s]
            nc.vector.quantize_mx(
                out=codes[:].rearrange("p g a w -> p (g a w)").bitcast(FP8X4),
                scales=scales[:].rearrange("p g a w -> p (g a w)"),
                in_=grouped[s][:].rearrange("p g n -> p (g n)"),
            )

        def quantise_pair(s, g):
            pair = [banks[s].get(g), banks[s].get(g + 1)]
            if None in pair or pair[0].shape[1] < MAX_TILES or pair[1].shape[1] < MAX_TILES:
                quantise(s, g)
                quantise(s, g + 1)
                return
            codes, scales = quantised[s]
            nc.vector.quantize_mx(
                out=codes[:, g : g + 2].rearrange("p g a w -> p (g a w)").bitcast(FP8X4),
                scales=scales[:, g : g + 2].rearrange("p g a w -> p (g a w)"),
                in_=grouped[s][:, g : g + 2, :].rearrange("p g n -> p (g n)"),
            )

        def multiply(bank, s, g, a, start, stop):
            codes, scales = quantised[s]
            nc.tensor.matmul_mx(
                out=bank[:],
                lhsT=codes[:, g, a, :].bitcast(FP8X4),
                lhsT_scale=scales[:, g, a, :],
                rhs=weights[g][0][:].bitcast(FP8X4),
                rhs_scale=weights[g][1][:],
                start=start,
                stop=stop,
            )

        def gate_passes(u, tiles=slice(0, MAX_TILES)):
            if not in_range(u):
                return
            gate_banks.setdefault(u, [])
            for a in range(UNIT_TILES[u])[tiles]:
                bank = psum.tile([P, WIDTH], F32, tag="bank")
                gate_banks[u].append(bank)
                for g in range(GATE_INPUTS):
                    multiply(bank, u, g, a, start=(g == 0), stop=(g == GATE_INPUTS - 1))

        def gate_sigmoid(u):
            if not in_range(u):
                return
            gate_sb = stage.tile([P, UNIT_TILES[u], WIDTH], F32)
            gates[u] = gate_sb
            if u in STORE_FIRST:
                open_store["ht"] = stage.tile([P, STORE_TILES[u], WIDTH], F32, name="ht", bufs=17)
            hidden[u] = (open_store["ht"], UNIT_START[u] - UNIT_START[STORE_OF[u]])
            for a, bank in enumerate(gate_banks[u]):
                nc.scalar.activation(out=gate_sb[:, a, :], in_=bank[:], func=ACT.Sigmoid)
            if vector_columns(u) < UNIT_TILES[u] * WIDTH:
                nc.gpsimd.tensor_tensor(
                    out=flat(hidden_rows(u))[:, vector_columns(u) :],
                    in0=flat(gate_sb[:])[:, vector_columns(u) :],
                    in1=flat(tanh_cell[u][:])[:, vector_columns(u) :],
                    op=MULT,
                )

        def first_product(u):
            if not in_range(u) or vector_columns(u) == 0:
                return
            nc.vector.tensor_tensor(
                out=flat(hidden_rows(u))[:, : vector_columns(u)],
                in0=flat(gates[u][:])[:, : vector_columns(u)],
                in1=flat(tanh_cell[u][:])[:, : vector_columns(u)],
                op=MULT,
            )

        def round_hidden(u):
            if not in_range(u):
                return
            ht16 = stage.tile([P, UNIT_TILES[u], WIDTH], BF16, bufs=2)
            rounded_hidden[u] = ht16
            nc.vector.tensor_copy(out=ht16[:], in_=hidden_rows(u))
            if u in STORE_LAST:
                nc.sync.dma_start(out=ht_dram[:, store_tiles(u), :], in_=hidden[u][0][:])

        def readout_passes(u):
            if not in_range(u):
                return
            readout_banks[u] = []
            for a in range(UNIT_TILES[u]):
                bank = psum.tile([P, WIDTH], F32, tag="bank")
                readout_banks[u].append(bank)
                multiply(bank, u + HIDDEN_LAG, HIDDEN, a, start=True, stop=True)

        def keep_warm(count):
            bank = psum.tile([P, WIDTH], F32, tag="bank")
            for i in range(count):
                nc.tensor.matmul(out=bank[:], lhsT=zeros[:, :P], rhs=zeros[:], start=True, stop=True)

        def readout_sigmoid(u):
            if not in_range(u):
                return
            if u in STORE_FIRST:
                open_store["yt"] = stage.tile([P, STORE_TILES[u], WIDTH], F32, name="yt", bufs=6)
            first = UNIT_START[u] - UNIT_START[STORE_OF[u]]
            for a, bank in enumerate(readout_banks[u]):
                nc.scalar.activation(out=open_store["yt"][:, first + a, :], in_=bank[:], func=ACT.Sigmoid)
                if u >= UNITS - 4:
                    nc.sync.dma_start(out=yt_dram[:, UNIT_START[u] + a : UNIT_START[u] + a + 1, :], in_=open_store["yt"][:, a : a + 1, :])
            if u in STORE_LAST and u < UNITS - 4:
                nc.sync.dma_start(out=yt_dram[:, store_tiles(u), :], in_=open_store["yt"][:])

        def step(s):
            for j in range(LOADS):
                if in_range(s) and j not in issued and LOAD_START[j] < UNIT_START[s] + PREFETCH:
                    issued.add(j)
                    load(j)
            transpose_operands(s, range(OPERANDS))
            open_step(s)
            tanh(s)
            first_product(s - 2)
            regroup(s, CELL, nc.scalar.copy)
            regroup(s, 0, nc.vector.tensor_copy)
            regroup(s, 1, nc.vector.tensor_copy)
            regroup(s, HIDDEN, nc.vector.tensor_copy)
            quantise_pair(s, 0)
            round_hidden(s - 2)
            quantise_pair(s, CELL)
            gate_passes(s - 1)
            readout_passes(s - 1 - HIDDEN_LAG)
            gate_sigmoid(s - 1)
            readout_sigmoid(s - 1 - HIDDEN_LAG)

        zeros = keep.tile([P, WIDTH], BF16)
        nc.gpsimd.memset(zeros[:], 0.0)
        zero = keep.tile([P, 1], F32)
        nc.vector.memset(zero[:], 0.0)
        warm = keep.tile([P, 1], F32)
        nc.scalar.activation(out=warm[:], in_=zero[:], func=ACT.Sigmoid)
        identity = keep.tile([P, P], F32)
        make_identity(nc, identity[:])

        raw[0] = load_weight((w_ip_o, w_output, w_output_c, w_op)[0])
        raw[1] = load_weight((w_ip_o, w_output, w_output_c, w_op)[1])
        raw[2] = load_weight((w_ip_o, w_output, w_output_c, w_op)[2])
        load(0)
        load(1)
        raw[3] = load_weight((w_ip_o, w_output, w_output_c, w_op)[3])
        issued.update((0, 1,))
        regroup_weight(0)
        regroup_weight(1)
        quantise_weight(0)
        regroup_weight(2)
        quantise_weight(1)
        quantise_weight(2)
        step(0)
        step(1)
        regroup_weight(3)
        step(2)
        quantise_weight(3)
        for s in range(3, UNITS + HIDDEN_LAG + 1):
            step(s)
